import numpy as np
import ml_dtypes

BF16 = ml_dtypes.bfloat16


def bf(x):
    return np.asarray(x, np.float32).astype(BF16)


def f32(x):
    return np.asarray(x, np.float32)


def f64(x):
    return np.asarray(x).astype(np.float64)


def striped(idx):
    return np.tile(idx.reshape(-1, 16).T, (8, 1))


V, D, H, B, N = 512, 128, 256, 128, 256


def sigmoid(v):
    return 1.0 / (1.0 + np.exp(-v))


def draw_w():
    return bf(np.random.standard_normal((D, H)) / np.sqrt(D))


def draw_b():
    return f32(0.3 * np.random.standard_normal((H, 1)))


def cell(x, wi, bi, wc, bc, wo, bo):
    gi = f64(wi).T @ x + f64(bi)
    gc = f64(wc).T @ x + f64(bc)
    go = f64(wo).T @ x + f64(bo)
    return sigmoid(go) * np.tanh(sigmoid(gi) * np.tanh(gc))


def setup_inputs():
    return {"table": bf(np.random.standard_normal((D, V))), "wi_fw": draw_w(), "bi_fw": draw_b(), "wc_fw": draw_w(), "bc_fw": draw_b(), "wo_fw": draw_w(), "bo_fw": draw_b(), "wi_bw": draw_w(), "bi_bw": draw_b(), "wc_bw": draw_w(), "bc_bw": draw_b(), "wo_bw": draw_w(), "bo_bw": draw_b(), "offs": striped(np.random.permutation(np.tile(np.arange(V), 2))[:N])}


def reference(table, wi_fw, bi_fw, wc_fw, bc_fw, wo_fw, bo_fw, wi_bw, bi_bw, wc_bw, bc_bw, wo_bw, bo_bw, offs):
    idx = offs[:16].T.reshape(-1)
    x = f64(table)[:, idx]
    y_fw = cell(x[:, :B], wi_fw, bi_fw, wc_fw, bc_fw, wo_fw, bo_fw)
    y_bw = cell(x[:, B:], wi_bw, bi_bw, wc_bw, bc_bw, wo_bw, bo_bw)
    return y_fw + y_bw

@@ -1,0 +1,80 @@
+import concourse.mybir as mybir
+
+P = 128
+V = 512
+H = 256
+B = 128
+DIRECTIONS = 2
+GATES = 3
+FLOPS = 2 * P * H * GATES * DIRECTIONS * B
+
+BF16, F32, U16 = mybir.dt.bfloat16, mybir.dt.float32, mybir.dt.uint16
+SIGMOID = mybir.ActivationFunctionType.Sigmoid
+TANH = mybir.ActivationFunctionType.Tanh
+
+
+def tile_textbilstm_kernel(
+    tc,
+    table, wi_fw, bi_fw, wc_fw, bc_fw, wo_fw, bo_fw, wi_bw, bi_bw, wc_bw, bc_bw, wo_bw, bo_bw, offs,
+    out,
+):
+    nc = tc.nc
+    cells = (
+        ((wi_fw, bi_fw), (wc_fw, bc_fw), (wo_fw, bo_fw)),
+        ((wi_bw, bi_bw), (wc_bw, bc_bw), (wo_bw, bo_bw)),
+    )
+    with (
+        tc.tile_pool(name="held", bufs=1) as held,
+        tc.tile_pool(name="work", bufs=2) as work,
+        tc.psum_pool(name="psum", bufs=4) as psum,
+    ):
+        offsets = held.tile([P, DIRECTIONS * B // 16], U16, name="offsets")
+        nc.sync.dma_start(offsets[:], offs)
+        words = held.tile([P, V], BF16, name="words")
+        nc.scalar.dma_start(words[:], table)
+        weights = []
+        biases = []
+        for d in range(DIRECTIONS):
+            for g in range(GATES):
+                w_dram, b_dram = cells[d][g]
+                weight = held.tile([P, H], BF16, name=f"weight{d}{g}")
+                (nc.sync if g % 2 == 0 else nc.scalar).dma_start(weight[:], w_dram)
+                weights.append(weight)
+                bias = held.tile([P, H // P], F32, name=f"bias{d}{g}")
+                with nc.allow_non_contiguous_dma(reason="a bias of 256 numbers, one to a partition"):
+                    (nc.scalar if g % 2 == 0 else nc.sync).dma_start(
+                        bias[:], b_dram.rearrange("(k p) o -> p (k o)", p=P)
+                    )
+                biases.append(bias)
+
+        forward = []
+        for d in range(DIRECTIONS):
+            for k in range(H // P):
+                gates = psum.tile([P, GATES, B], F32, name="gates")
+                for g in range(GATES):
+                    looked_up = words[:].indirect(offsets[:, d * (B // 16) : (d + 1) * (B // 16)])
+                    nc.tensor.matmul(
+                        gates[:, g, :], weights[d * GATES + g][:, k * P : (k + 1) * P], looked_up,
+                        start=True, stop=True,
+                    )
+                bias_i, bias_c, bias_o = (biases[d * GATES + g][:, k : k + 1] for g in range(GATES))
+                gate_i = work.tile([P, B], F32, name="gate_i")
+                nc.scalar.activation(gate_i[:], gates[:, 0, :], SIGMOID, bias=bias_i)
+                candidate = work.tile([P, B], F32, name="candidate")
+                nc.scalar.activation(candidate[:], gates[:, 1, :], TANH, bias=bias_c)
+                state = work.tile([P, B], F32, name="state")
+                nc.vector.tensor_mul(state[:], gate_i[:], candidate[:])
+                gate_o = work.tile([P, B], F32, name="gate_o")
+                nc.scalar.activation(gate_o[:], gates[:, 2, :], SIGMOID, bias=bias_o)
+                squashed = work.tile([P, B], F32, name="squashed")
+                nc.scalar.activation(squashed[:], state[:], TANH)
+                if d == 0:
+                    hidden = work.tile([P, B], F32, name="hidden_fw")
+                    nc.vector.tensor_mul(hidden[:], gate_o[:], squashed[:])
+                    forward.append(hidden)
+                else:
+                    hidden = work.tile([P, B], F32, name="hidden_bw")
+                    nc.vector.tensor_mul(hidden[:], gate_o[:], squashed[:])
+                    both = work.tile([P, B], F32, name="both")
+                    nc.vector.tensor_add(both[:], forward[k][:], hidden[:])
+                    nc.sync.dma_start(out[k * P : (k + 1) * P, :], both[:])

@@ -6,6 +6,7 @@ H = 256
 B = 128
 DIRECTIONS = 2
 GATES = 3
+WARMING = 5
 FLOPS = 2 * P * H * GATES * DIRECTIONS * B
 
 BF16, F32, U16 = mybir.dt.bfloat16, mybir.dt.float32, mybir.dt.uint16
@@ -46,6 +47,12 @@ def tile_textbilstm_kernel(
                         bias[:], b_dram.rearrange("(k p) o -> p (k o)", p=P)
                     )
                 biases.append(bias)
+
+        zeros = held.tile([P, V], BF16, name="zeros")
+        nc.vector.memset(zeros[:], 0.0)
+        unused = psum.tile([P, V], F32, name="unused")
+        for i in range(WARMING):
+            nc.tensor.matmul(unused[:], zeros[:, 0:P], zeros[:], start=True, stop=True)
 
         forward = []
         for d in range(DIRECTIONS):

@@ -6,7 +6,6 @@ H = 256
 B = 128
 DIRECTIONS = 2
 GATES = 3
-WARMING = 5
 FLOPS = 2 * P * H * GATES * DIRECTIONS * B
 
 BF16, F32, U16 = mybir.dt.bfloat16, mybir.dt.float32, mybir.dt.uint16
@@ -48,11 +47,9 @@ def tile_textbilstm_kernel(
                     )
                 biases.append(bias)
 
-        zeros = held.tile([P, V], BF16, name="zeros")
-        nc.vector.memset(zeros[:], 0.0)
-        unused = psum.tile([P, V], F32, name="unused")
-        for i in range(WARMING):
-            nc.tensor.matmul(unused[:], zeros[:, 0:P], zeros[:], start=True, stop=True)
+        primer = held.tile([P, 1], F32, name="primer")
+        nc.vector.memset(primer[:], 0.0)
+        nc.scalar.activation(primer[:], primer[:], SIGMOID)
 
         forward = []
         for d in range(DIRECTIONS):

@@ -47,11 +47,23 @@ def tile_textbilstm_kernel(
                     )
                 biases.append(bias)
 
-        primer = held.tile([P, 1], F32, name="primer")
-        nc.vector.memset(primer[:], 0.0)
-        nc.scalar.activation(primer[:], primer[:], SIGMOID)
-
         forward = []
+
+        def finish(d, k, state, gate_o):
+            squashed = work.tile([P, B], F32, name="squashed")
+            nc.scalar.activation(squashed[:], state[:], TANH)
+            if d == 0:
+                hidden = work.tile([P, B], F32, name="hidden_fw")
+                nc.vector.tensor_mul(hidden[:], gate_o[:], squashed[:])
+                forward.append(hidden)
+            else:
+                hidden = work.tile([P, B], F32, name="hidden_bw")
+                nc.vector.tensor_mul(hidden[:], gate_o[:], squashed[:])
+                both = work.tile([P, B], F32, name="both")
+                nc.vector.tensor_add(both[:], forward[k][:], hidden[:])
+                nc.sync.dma_start(out[k * P : (k + 1) * P, :], both[:])
+
+        waiting = None
         for d in range(DIRECTIONS):
             for k in range(H // P):
                 gates = psum.tile([P, GATES, B], F32, name="gates")
@@ -68,17 +80,9 @@ def tile_textbilstm_kernel(
                 nc.scalar.activation(candidate[:], gates[:, 1, :], TANH, bias=bias_c)
                 state = work.tile([P, B], F32, name="state")
                 nc.vector.tensor_mul(state[:], gate_i[:], candidate[:])
+                if waiting is not None:
+                    finish(*waiting)
                 gate_o = work.tile([P, B], F32, name="gate_o")
                 nc.scalar.activation(gate_o[:], gates[:, 2, :], SIGMOID, bias=bias_o)
-                squashed = work.tile([P, B], F32, name="squashed")
-                nc.scalar.activation(squashed[:], state[:], TANH)
-                if d == 0:
-                    hidden = work.tile([P, B], F32, name="hidden_fw")
-                    nc.vector.tensor_mul(hidden[:], gate_o[:], squashed[:])
-                    forward.append(hidden)
-                else:
-                    hidden = work.tile([P, B], F32, name="hidden_bw")
-                    nc.vector.tensor_mul(hidden[:], gate_o[:], squashed[:])
-                    both = work.tile([P, B], F32, name="both")
-                    nc.vector.tensor_add(both[:], forward[k][:], hidden[:])
-                    nc.sync.dma_start(out[k * P : (k + 1) * P, :], both[:])
+                waiting = (d, k, state, gate_o)
+        finish(*waiting)

@@ -1,4 +1,5 @@
 import concourse.mybir as mybir
+from concourse.masks import make_identity
 
 P = 128
 V = 512
@@ -6,6 +7,8 @@ H = 256
 B = 128
 DIRECTIONS = 2
 GATES = 3
+BLOCKS = H // P
+ROWS = GATES * BLOCKS
 FLOPS = 2 * P * H * GATES * DIRECTIONS * B
 
 BF16, F32, U16 = mybir.dt.bfloat16, mybir.dt.float32, mybir.dt.uint16
@@ -27,45 +30,39 @@ def tile_textbilstm_kernel(
         tc.tile_pool(name="held", bufs=1) as held,
         tc.tile_pool(name="work", bufs=2) as work,
         tc.psum_pool(name="psum", bufs=4) as psum,
+        tc.psum_pool(name="psum_bias", bufs=2) as psum_bias,
     ):
         offsets = held.tile([P, DIRECTIONS * B // 16], U16, name="offsets")
         nc.sync.dma_start(offsets[:], offs)
         words = held.tile([P, V], BF16, name="words")
         nc.scalar.dma_start(words[:], table)
         weights = []
-        biases = []
+        bias_rows = []
         for d in range(DIRECTIONS):
+            rows = held.tile([ROWS, P], F32, name=f"rows{d}")
+            bias_rows.append(rows)
             for g in range(GATES):
                 w_dram, b_dram = cells[d][g]
                 weight = held.tile([P, H], BF16, name=f"weight{d}{g}")
                 (nc.sync if g % 2 == 0 else nc.scalar).dma_start(weight[:], w_dram)
                 weights.append(weight)
-                bias = held.tile([P, H // P], F32, name=f"bias{d}{g}")
-                with nc.allow_non_contiguous_dma(reason="a bias of 256 numbers, one to a partition"):
-                    (nc.scalar if g % 2 == 0 else nc.sync).dma_start(
-                        bias[:], b_dram.rearrange("(k p) o -> p (k o)", p=P)
-                    )
-                biases.append(bias)
+                (nc.scalar if g % 2 == 0 else nc.sync).dma_start(
+                    rows[g * BLOCKS : (g + 1) * BLOCKS, :], b_dram.rearrange("(k p) o -> k (p o)", p=P)
+                )
+
+        identity = held.tile([ROWS, ROWS], F32, name="identity")
+        make_identity(nc, identity[:])
+        biases = []
+        for d in range(DIRECTIONS):
+            turned = psum_bias.tile([P, ROWS], F32, name="turned")
+            nc.tensor.matmul(turned[:], bias_rows[d][:], identity[:], start=True, stop=True)
+            bias = held.tile([P, ROWS], F32, name=f"bias{d}")
+            nc.vector.tensor_copy(bias[:], turned[:])
+            biases.append(bias)
 
         forward = []
-
-        def finish(d, k, state, gate_o):
-            squashed = work.tile([P, B], F32, name="squashed")
-            nc.scalar.activation(squashed[:], state[:], TANH)
-            if d == 0:
-                hidden = work.tile([P, B], F32, name="hidden_fw")
-                nc.vector.tensor_mul(hidden[:], gate_o[:], squashed[:])
-                forward.append(hidden)
-            else:
-                hidden = work.tile([P, B], F32, name="hidden_bw")
-                nc.vector.tensor_mul(hidden[:], gate_o[:], squashed[:])
-                both = work.tile([P, B], F32, name="both")
-                nc.vector.tensor_add(both[:], forward[k][:], hidden[:])
-                nc.sync.dma_start(out[k * P : (k + 1) * P, :], both[:])
-
-        waiting = None
         for d in range(DIRECTIONS):
-            for k in range(H // P):
+            for k in range(BLOCKS):
                 gates = psum.tile([P, GATES, B], F32, name="gates")
                 for g in range(GATES):
                     looked_up = words[:].indirect(offsets[:, d * (B // 16) : (d + 1) * (B // 16)])
@@ -73,16 +70,26 @@ def tile_textbilstm_kernel(
                         gates[:, g, :], weights[d * GATES + g][:, k * P : (k + 1) * P], looked_up,
                         start=True, stop=True,
                     )
-                bias_i, bias_c, bias_o = (biases[d * GATES + g][:, k : k + 1] for g in range(GATES))
+                bias_i, bias_c, bias_o = (
+                    biases[d][:, g * BLOCKS + k : g * BLOCKS + k + 1] for g in range(GATES)
+                )
                 gate_i = work.tile([P, B], F32, name="gate_i")
                 nc.scalar.activation(gate_i[:], gates[:, 0, :], SIGMOID, bias=bias_i)
                 candidate = work.tile([P, B], F32, name="candidate")
                 nc.scalar.activation(candidate[:], gates[:, 1, :], TANH, bias=bias_c)
                 state = work.tile([P, B], F32, name="state")
                 nc.vector.tensor_mul(state[:], gate_i[:], candidate[:])
-                if waiting is not None:
-                    finish(*waiting)
                 gate_o = work.tile([P, B], F32, name="gate_o")
                 nc.scalar.activation(gate_o[:], gates[:, 2, :], SIGMOID, bias=bias_o)
-                waiting = (d, k, state, gate_o)
-        finish(*waiting)
+                squashed = work.tile([P, B], F32, name="squashed")
+                nc.scalar.activation(squashed[:], state[:], TANH)
+                if d == 0:
+                    hidden = work.tile([P, B], F32, name="hidden_fw")
+                    nc.vector.tensor_mul(hidden[:], gate_o[:], squashed[:])
+                    forward.append(hidden)
+                else:
+                    hidden = work.tile([P, B], F32, name="hidden_bw")
+                    nc.vector.tensor_mul(hidden[:], gate_o[:], squashed[:])
+                    both = work.tile([P, B], F32, name="both")
+                    nc.vector.tensor_add(both[:], forward[k][:], hidden[:])
+                    nc.sync.dma_start(out[k * P : (k + 1) * P, :], both[:])

@@ -1,5 +1,4 @@
 import concourse.mybir as mybir
-from concourse.masks import make_identity
 
 P = 128
 V = 512
@@ -7,8 +6,6 @@ H = 256
 B = 128
 DIRECTIONS = 2
 GATES = 3
-BLOCKS = H // P
-ROWS = GATES * BLOCKS
 FLOPS = 2 * P * H * GATES * DIRECTIONS * B
 
 BF16, F32, U16 = mybir.dt.bfloat16, mybir.dt.float32, mybir.dt.uint16
@@ -30,39 +27,31 @@ def tile_textbilstm_kernel(
         tc.tile_pool(name="held", bufs=1) as held,
         tc.tile_pool(name="work", bufs=2) as work,
         tc.psum_pool(name="psum", bufs=4) as psum,
-        tc.psum_pool(name="psum_bias", bufs=2) as psum_bias,
     ):
         offsets = held.tile([P, DIRECTIONS * B // 16], U16, name="offsets")
         nc.sync.dma_start(offsets[:], offs)
         words = held.tile([P, V], BF16, name="words")
         nc.scalar.dma_start(words[:], table)
         weights = []
-        bias_rows = []
+        biases = []
         for d in range(DIRECTIONS):
-            rows = held.tile([ROWS, P], F32, name=f"rows{d}")
-            bias_rows.append(rows)
             for g in range(GATES):
                 w_dram, b_dram = cells[d][g]
                 weight = held.tile([P, H], BF16, name=f"weight{d}{g}")
-                (nc.sync if g % 2 == 0 else nc.scalar).dma_start(weight[:], w_dram)
+                nc.sync.dma_start(weight[:], w_dram)
                 weights.append(weight)
-                (nc.scalar if g % 2 == 0 else nc.sync).dma_start(
-                    rows[g * BLOCKS : (g + 1) * BLOCKS, :], b_dram.rearrange("(k p) o -> k (p o)", p=P)
-                )
+                bias = held.tile([P, H // P], F32, name=f"bias{d}{g}")
+                with nc.allow_non_contiguous_dma(reason="a bias of 256 numbers, one to a partition"):
+                    nc.sync.dma_start(bias[:], b_dram.rearrange("(k p) o -> p (k o)", p=P))
+                biases.append(bias)
 
-        identity = held.tile([ROWS, ROWS], F32, name="identity")
-        make_identity(nc, identity[:])
-        biases = []
-        for d in range(DIRECTIONS):
-            turned = psum_bias.tile([P, ROWS], F32, name="turned")
-            nc.tensor.matmul(turned[:], bias_rows[d][:], identity[:], start=True, stop=True)
-            bias = held.tile([P, ROWS], F32, name=f"bias{d}")
-            nc.vector.tensor_copy(bias[:], turned[:])
-            biases.append(bias)
+        primer = held.tile([P, 1], F32, name="primer")
+        nc.gpsimd.memset(primer[:], 0.0)
+        nc.scalar.activation(primer[:], primer[:], SIGMOID)
 
         forward = []
         for d in range(DIRECTIONS):
-            for k in range(BLOCKS):
+            for k in range(H // P):
                 gates = psum.tile([P, GATES, B], F32, name="gates")
                 for g in range(GATES):
                     looked_up = words[:].indirect(offsets[:, d * (B // 16) : (d + 1) * (B // 16)])
@@ -70,9 +59,7 @@ def tile_textbilstm_kernel(
                         gates[:, g, :], weights[d * GATES + g][:, k * P : (k + 1) * P], looked_up,
                         start=True, stop=True,
                     )
-                bias_i, bias_c, bias_o = (
-                    biases[d][:, g * BLOCKS + k : g * BLOCKS + k + 1] for g in range(GATES)
-                )
+                bias_i, bias_c, bias_o = (biases[d * GATES + g][:, k : k + 1] for g in range(GATES))
                 gate_i = work.tile([P, B], F32, name="gate_i")
                 nc.scalar.activation(gate_i[:], gates[:, 0, :], SIGMOID, bias=bias_i)
                 candidate = work.tile([P, B], F32, name="candidate")

@@ -3,14 +3,16 @@ import concourse.mybir as mybir
 P = 128
 V = 512
 H = 256
+BLOCKS = H // P
 B = 128
-DIRECTIONS = 2
-GATES = 3
-FLOPS = 2 * P * H * GATES * DIRECTIONS * B
+FORWARD, BACKWARD = 0, 1
+INPUT, CANDIDATE, OUTPUT = 0, 1, 2
+FLOPS = 2 * P * H * 3 * 2 * B
 
 BF16, F32, U16 = mybir.dt.bfloat16, mybir.dt.float32, mybir.dt.uint16
 SIGMOID = mybir.ActivationFunctionType.Sigmoid
 TANH = mybir.ActivationFunctionType.Tanh
+FUNCTION = {INPUT: SIGMOID, CANDIDATE: TANH, OUTPUT: SIGMOID}
 
 
 def tile_textbilstm_kernel(
@@ -19,64 +21,71 @@ def tile_textbilstm_kernel(
     out,
 ):
     nc = tc.nc
-    cells = (
-        ((wi_fw, bi_fw), (wc_fw, bc_fw), (wo_fw, bo_fw)),
-        ((wi_bw, bi_bw), (wc_bw, bc_bw), (wo_bw, bo_bw)),
-    )
+    in_dram = {
+        (FORWARD, INPUT): (wi_fw, bi_fw), (FORWARD, CANDIDATE): (wc_fw, bc_fw), (FORWARD, OUTPUT): (wo_fw, bo_fw),
+        (BACKWARD, INPUT): (wi_bw, bi_bw), (BACKWARD, CANDIDATE): (wc_bw, bc_bw), (BACKWARD, OUTPUT): (wo_bw, bo_bw),
+    }
     with (
         tc.tile_pool(name="held", bufs=1) as held,
         tc.tile_pool(name="work", bufs=2) as work,
-        tc.psum_pool(name="psum", bufs=4) as psum,
+        tc.psum_pool(name="psum", bufs=2) as psum,
     ):
-        offsets = held.tile([P, DIRECTIONS * B // 16], U16, name="offsets")
+        offsets = held.tile([P, 2 * B // 16], U16, name="offsets")
         nc.sync.dma_start(offsets[:], offs)
         words = held.tile([P, V], BF16, name="words")
         nc.scalar.dma_start(words[:], table)
-        weights = []
-        biases = []
-        for d in range(DIRECTIONS):
-            for g in range(GATES):
-                w_dram, b_dram = cells[d][g]
-                weight = held.tile([P, H], BF16, name=f"weight{d}{g}")
-                nc.sync.dma_start(weight[:], w_dram)
-                weights.append(weight)
-                bias = held.tile([P, H // P], F32, name=f"bias{d}{g}")
+        weights = {}
+        biases = {}
+        for d in (FORWARD, BACKWARD):
+            for g in (INPUT, CANDIDATE, OUTPUT):
+                w_dram, b_dram = in_dram[(d, g)]
+                weights[(d, g)] = held.tile([P, H], BF16, name=f"weight{d}{g}")
+                nc.sync.dma_start(weights[(d, g)][:], w_dram)
+                biases[(d, g)] = held.tile([P, BLOCKS], F32, name=f"bias{d}{g}")
                 with nc.allow_non_contiguous_dma(reason="a bias of 256 numbers, one to a partition"):
-                    nc.sync.dma_start(bias[:], b_dram.rearrange("(k p) o -> p (k o)", p=P))
-                biases.append(bias)
+                    nc.sync.dma_start(biases[(d, g)][:], b_dram.rearrange("(k p) o -> p (k o)", p=P))
 
         primer = held.tile([P, 1], F32, name="primer")
         nc.gpsimd.memset(primer[:], 0.0)
         nc.scalar.activation(primer[:], primer[:], SIGMOID)
 
-        forward = []
-        for d in range(DIRECTIONS):
-            for k in range(H // P):
-                gates = psum.tile([P, GATES, B], F32, name="gates")
-                for g in range(GATES):
-                    looked_up = words[:].indirect(offsets[:, d * (B // 16) : (d + 1) * (B // 16)])
-                    nc.tensor.matmul(
-                        gates[:, g, :], weights[d * GATES + g][:, k * P : (k + 1) * P], looked_up,
-                        start=True, stop=True,
-                    )
-                bias_i, bias_c, bias_o = (biases[d * GATES + g][:, k : k + 1] for g in range(GATES))
-                gate_i = work.tile([P, B], F32, name="gate_i")
-                nc.scalar.activation(gate_i[:], gates[:, 0, :], SIGMOID, bias=bias_i)
-                candidate = work.tile([P, B], F32, name="candidate")
-                nc.scalar.activation(candidate[:], gates[:, 1, :], TANH, bias=bias_c)
-                state = work.tile([P, B], F32, name="state")
-                nc.vector.tensor_mul(state[:], gate_i[:], candidate[:])
-                gate_o = work.tile([P, B], F32, name="gate_o")
-                nc.scalar.activation(gate_o[:], gates[:, 2, :], SIGMOID, bias=bias_o)
-                squashed = work.tile([P, B], F32, name="squashed")
-                nc.scalar.activation(squashed[:], state[:], TANH)
-                if d == 0:
-                    hidden = work.tile([P, B], F32, name="hidden_fw")
-                    nc.vector.tensor_mul(hidden[:], gate_o[:], squashed[:])
-                    forward.append(hidden)
+        def project(bank_columns, d, g, k):
+            looked_up = words[:].indirect(offsets[:, d * (B // 16) : (d + 1) * (B // 16)])
+            nc.tensor.matmul(bank_columns, weights[(d, g)][:, k * P : (k + 1) * P], looked_up, start=True, stop=True)
+
+        def squash(bank_columns, d, g, k):
+            gate = work.tile([P, B], F32, name=f"gate{g}{k}")
+            nc.scalar.activation(gate[:], bank_columns, FUNCTION[g], bias=biases[(d, g)][:, k : k + 1])
+            return gate
+
+        forward = {}
+        for d in (FORWARD, BACKWARD):
+            first = psum.tile([P, BLOCKS, B], F32, name="first")
+            for k in range(BLOCKS):
+                project(first[:, k, :], d, INPUT, k)
+            second = psum.tile([P, 2, BLOCKS, B], F32, name="second")
+            for g in (CANDIDATE, OUTPUT):
+                for k in range(BLOCKS):
+                    project(second[:, g - CANDIDATE, k, :], d, g, k)
+            gates_i = {}
+            for k in range(BLOCKS):
+                gates_i[k] = squash(first[:, k, :], d, INPUT, k)
+            states = {}
+            for k in range(BLOCKS):
+                candidate = squash(second[:, 0, k, :], d, CANDIDATE, k)
+                states[k] = work.tile([P, B], F32, name=f"state{k}")
+                nc.vector.tensor_mul(states[k][:], gates_i[k][:], candidate[:])
+            gates_o = {}
+            for k in range(BLOCKS):
+                gates_o[k] = squash(second[:, 1, k, :], d, OUTPUT, k)
+            for k in range(BLOCKS):
+                squashed = work.tile([P, B], F32, name=f"squashed{k}")
+                nc.scalar.activation(squashed[:], states[k][:], TANH)
+                hidden = work.tile([P, B], F32, name=f"hidden{k}")
+                nc.vector.tensor_mul(hidden[:], gates_o[k][:], squashed[:])
+                if d == FORWARD:
+                    forward[k] = hidden
                 else:
-                    hidden = work.tile([P, B], F32, name="hidden_bw")
-                    nc.vector.tensor_mul(hidden[:], gate_o[:], squashed[:])
-                    both = work.tile([P, B], F32, name="both")
+                    both = work.tile([P, B], F32, name=f"both{k}")
                     nc.vector.tensor_add(both[:], forward[k][:], hidden[:])
                     nc.sync.dma_start(out[k * P : (k + 1) * P, :], both[:])

@@ -25,10 +25,13 @@ def tile_textbilstm_kernel(
         (FORWARD, INPUT): (wi_fw, bi_fw), (FORWARD, CANDIDATE): (wc_fw, bc_fw), (FORWARD, OUTPUT): (wo_fw, bo_fw),
         (BACKWARD, INPUT): (wi_bw, bi_bw), (BACKWARD, CANDIDATE): (wc_bw, bc_bw), (BACKWARD, OUTPUT): (wo_bw, bo_bw),
     }
+    order = (
+        (FORWARD, INPUT), (FORWARD, CANDIDATE), (BACKWARD, INPUT), (BACKWARD, CANDIDATE),
+        (FORWARD, OUTPUT), (BACKWARD, OUTPUT),
+    )
     with (
         tc.tile_pool(name="held", bufs=1) as held,
-        tc.tile_pool(name="work", bufs=2) as work,
-        tc.psum_pool(name="psum", bufs=2) as psum,
+        tc.psum_pool(name="psum", bufs=1) as psum,
     ):
         offsets = held.tile([P, 2 * B // 16], U16, name="offsets")
         nc.sync.dma_start(offsets[:], offs)
@@ -36,56 +39,71 @@ def tile_textbilstm_kernel(
         nc.scalar.dma_start(words[:], table)
         weights = {}
         biases = {}
-        for d in (FORWARD, BACKWARD):
-            for g in (INPUT, CANDIDATE, OUTPUT):
-                w_dram, b_dram = in_dram[(d, g)]
-                weights[(d, g)] = held.tile([P, H], BF16, name=f"weight{d}{g}")
-                nc.sync.dma_start(weights[(d, g)][:], w_dram)
-                biases[(d, g)] = held.tile([P, BLOCKS], F32, name=f"bias{d}{g}")
-                with nc.allow_non_contiguous_dma(reason="a bias of 256 numbers, one to a partition"):
-                    nc.sync.dma_start(biases[(d, g)][:], b_dram.rearrange("(k p) o -> p (k o)", p=P))
+        for d, g in order:
+            w_dram, b_dram = in_dram[(d, g)]
+            weights[(d, g)] = held.tile([P, H], BF16, name=f"weight{d}{g}")
+            nc.sync.dma_start(weights[(d, g)][:], w_dram)
+            biases[(d, g)] = held.tile([P, BLOCKS], F32, name=f"bias{d}{g}")
+            with nc.allow_non_contiguous_dma(reason="a bias of 256 numbers, one to a partition"):
+                nc.sync.dma_start(biases[(d, g)][:], b_dram.rearrange("(k p) o -> p (k o)", p=P))
 
         primer = held.tile([P, 1], F32, name="primer")
         nc.gpsimd.memset(primer[:], 0.0)
         nc.scalar.activation(primer[:], primer[:], SIGMOID)
 
-        def project(bank_columns, d, g, k):
-            looked_up = words[:].indirect(offsets[:, d * (B // 16) : (d + 1) * (B // 16)])
-            nc.tensor.matmul(bank_columns, weights[(d, g)][:, k * P : (k + 1) * P], looked_up, start=True, stop=True)
+        shared = psum.tile([P, 2, BLOCKS, B], F32, name="shared")
+        banks = {
+            (FORWARD, INPUT): psum.tile([P, BLOCKS, B], F32, name="bank_i_fw"),
+            (FORWARD, CANDIDATE): psum.tile([P, BLOCKS, B], F32, name="bank_c_fw"),
+            (BACKWARD, INPUT): psum.tile([P, BLOCKS, B], F32, name="bank_i_bw"),
+            (BACKWARD, CANDIDATE): shared[:, 0],
+            (FORWARD, OUTPUT): shared[:, 1],
+            (BACKWARD, OUTPUT): psum.tile([P, BLOCKS, B], F32, name="bank_o_bw"),
+        }
+        for d, g in order:
+            for k in range(BLOCKS):
+                looked_up = words[:].indirect(offsets[:, d * (B // 16) : (d + 1) * (B // 16)])
+                nc.tensor.matmul(
+                    banks[(d, g)][:, k, :], weights[(d, g)][:, k * P : (k + 1) * P], looked_up, start=True, stop=True
+                )
 
-        def squash(bank_columns, d, g, k):
-            gate = work.tile([P, B], F32, name=f"gate{g}{k}")
-            nc.scalar.activation(gate[:], bank_columns, FUNCTION[g], bias=biases[(d, g)][:, k : k + 1])
+        def squash(d, g):
+            gate = {}
+            for k in range(BLOCKS):
+                gate[k] = held.tile([P, B], F32, name=f"gate{d}{g}{k}")
+                nc.scalar.activation(
+                    gate[k][:], banks[(d, g)][:, k, :], FUNCTION[g], bias=biases[(d, g)][:, k : k + 1]
+                )
             return gate
 
-        forward = {}
-        for d in (FORWARD, BACKWARD):
-            first = psum.tile([P, BLOCKS, B], F32, name="first")
+        def product(name, left, right):
+            result = {}
             for k in range(BLOCKS):
-                project(first[:, k, :], d, INPUT, k)
-            second = psum.tile([P, 2, BLOCKS, B], F32, name="second")
-            for g in (CANDIDATE, OUTPUT):
-                for k in range(BLOCKS):
-                    project(second[:, g - CANDIDATE, k, :], d, g, k)
-            gates_i = {}
+                result[k] = held.tile([P, B], F32, name=f"{name}{k}")
+                nc.vector.tensor_mul(result[k][:], left[k][:], right[k][:])
+            return result
+
+        def tanh_of(name, state):
+            squashed = {}
             for k in range(BLOCKS):
-                gates_i[k] = squash(first[:, k, :], d, INPUT, k)
-            states = {}
-            for k in range(BLOCKS):
-                candidate = squash(second[:, 0, k, :], d, CANDIDATE, k)
-                states[k] = work.tile([P, B], F32, name=f"state{k}")
-                nc.vector.tensor_mul(states[k][:], gates_i[k][:], candidate[:])
-            gates_o = {}
-            for k in range(BLOCKS):
-                gates_o[k] = squash(second[:, 1, k, :], d, OUTPUT, k)
-            for k in range(BLOCKS):
-                squashed = work.tile([P, B], F32, name=f"squashed{k}")
-                nc.scalar.activation(squashed[:], states[k][:], TANH)
-                hidden = work.tile([P, B], F32, name=f"hidden{k}")
-                nc.vector.tensor_mul(hidden[:], gates_o[k][:], squashed[:])
-                if d == FORWARD:
-                    forward[k] = hidden
-                else:
-                    both = work.tile([P, B], F32, name=f"both{k}")
-                    nc.vector.tensor_add(both[:], forward[k][:], hidden[:])
-                    nc.sync.dma_start(out[k * P : (k + 1) * P, :], both[:])
+                squashed[k] = held.tile([P, B], F32, name=f"{name}{k}")
+                nc.scalar.activation(squashed[k][:], state[k][:], TANH)
+            return squashed
+
+        gate_i_fw = squash(FORWARD, INPUT)
+        candidate_fw = squash(FORWARD, CANDIDATE)
+        state_fw = product("state_fw", gate_i_fw, candidate_fw)
+        gate_i_bw = squash(BACKWARD, INPUT)
+        squashed_fw = tanh_of("squashed_fw", state_fw)
+        candidate_bw = squash(BACKWARD, CANDIDATE)
+        state_bw = product("state_bw", gate_i_bw, candidate_bw)
+        gate_o_fw = squash(FORWARD, OUTPUT)
+        hidden_fw = product("hidden_fw", gate_o_fw, squashed_fw)
+        squashed_bw = tanh_of("squashed_bw", state_bw)
+        gate_o_bw = squash(BACKWARD, OUTPUT)
+        hidden_bw = product("hidden_bw", gate_o_bw, squashed_bw)
+        hidden = {(FORWARD, 0): hidden_fw[0], (FORWARD, 1): hidden_fw[1], (BACKWARD, 0): hidden_bw[0], (BACKWARD, 1): hidden_bw[1]}
+        for k in range(BLOCKS):
+            both = held.tile([P, B], F32, name=f"both{k}")
+            nc.vector.tensor_add(both[:], hidden[(FORWARD, k)][:], hidden[(BACKWARD, k)][:])
+            nc.sync.dma_start(out[k * P : (k + 1) * P, :], both[:])

@@ -33,10 +33,10 @@ def tile_textbilstm_kernel(
         tc.tile_pool(name="held", bufs=1) as held,
         tc.psum_pool(name="psum", bufs=1) as psum,
     ):
+        words = held.tile([P, V], BF16, name="words")
+        nc.sync.dma_start(words[:], table)
         offsets = held.tile([P, 2 * B // 16], U16, name="offsets")
         nc.sync.dma_start(offsets[:], offs)
-        words = held.tile([P, V], BF16, name="words")
-        nc.scalar.dma_start(words[:], table)
         weights = {}
         biases = {}
         for d, g in order:

@@ -48,7 +48,7 @@ def tile_textbilstm_kernel(
                 nc.sync.dma_start(biases[(d, g)][:], b_dram.rearrange("(k p) o -> p (k o)", p=P))
 
         primer = held.tile([P, 1], F32, name="primer")
-        nc.gpsimd.memset(primer[:], 0.0)
+        nc.vector.memset(primer[:], 0.0)
         nc.scalar.activation(primer[:], primer[:], SIGMOID)
 
         shared = psum.tile([P, 2, BLOCKS, B], F32, name="shared")

@@ -44,8 +44,7 @@ def tile_textbilstm_kernel(
             weights[(d, g)] = held.tile([P, H], BF16, name=f"weight{d}{g}")
             nc.sync.dma_start(weights[(d, g)][:], w_dram)
             biases[(d, g)] = held.tile([P, BLOCKS], F32, name=f"bias{d}{g}")
-            with nc.allow_non_contiguous_dma(reason="a bias of 256 numbers, one to a partition"):
-                nc.sync.dma_start(biases[(d, g)][:], b_dram.rearrange("(k p) o -> p (k o)", p=P))
+            nc.sync.dma_start(biases[(d, g)][:], b_dram.rearrange("(p k) o -> p (k o)", p=P))
 
         primer = held.tile([P, 1], F32, name="primer")
         nc.vector.memset(primer[:], 0.0)
@@ -64,7 +63,7 @@ def tile_textbilstm_kernel(
             for k in range(BLOCKS):
                 looked_up = words[:].indirect(offsets[:, d * (B // 16) : (d + 1) * (B // 16)])
                 nc.tensor.matmul(
-                    banks[(d, g)][:, k, :], weights[(d, g)][:, k * P : (k + 1) * P], looked_up, start=True, stop=True
+                    banks[(d, g)][:, k, :], weights[(d, g)][:, k::BLOCKS], looked_up, start=True, stop=True
                 )
 
         def squash(d, g):
@@ -103,7 +102,8 @@ def tile_textbilstm_kernel(
         gate_o_bw = squash(BACKWARD, OUTPUT)
         hidden_bw = product("hidden_bw", gate_o_bw, squashed_bw)
         hidden = {(FORWARD, 0): hidden_fw[0], (FORWARD, 1): hidden_fw[1], (BACKWARD, 0): hidden_bw[0], (BACKWARD, 1): hidden_bw[1]}
+        out_by_block = out.rearrange("(p k) r -> p k r", p=P)
         for k in range(BLOCKS):
             both = held.tile([P, B], F32, name=f"both{k}")
             nc.vector.tensor_add(both[:], hidden[(FORWARD, k)][:], hidden[(BACKWARD, k)][:])
-            nc.sync.dma_start(out[k * P : (k + 1) * P, :], both[:])
+            nc.sync.dma_start(out_by_block[:, k, :], both[:])

@@ -7,6 +7,8 @@ BLOCKS = H // P
 B = 128
 FORWARD, BACKWARD = 0, 1
 INPUT, CANDIDATE, OUTPUT = 0, 1, 2
+WARM_REPEATS = 4
+WARM_MATMULS = 4
 FLOPS = 2 * P * H * 3 * 2 * B
 
 BF16, F32, U16 = mybir.dt.bfloat16, mybir.dt.float32, mybir.dt.uint16
@@ -45,6 +47,14 @@ def tile_textbilstm_kernel(
             nc.sync.dma_start(weights[(d, g)][:], w_dram)
             biases[(d, g)] = held.tile([P, BLOCKS], F32, name=f"bias{d}{g}")
             nc.sync.dma_start(biases[(d, g)][:], b_dram.rearrange("(p k) o -> p (k o)", p=P))
+
+        zeros = held.tile([P, P], BF16, name="zeros")
+        nc.vector.memset(zeros[:], 0.0)
+        warm = psum.tile([P, WARM_REPEATS, P], F32, name="warm")
+        for step in range(WARM_MATMULS):
+            nc.tensor.matmul(
+                warm[:], zeros[:], zeros[:].unsqueeze(1).to_broadcast([P, WARM_REPEATS, P]), start=True, stop=True
+            )
 
         primer = held.tile([P, 1], F32, name="primer")
         nc.vector.memset(primer[:], 0.0)

@@ -8,7 +8,7 @@ B = 128
 FORWARD, BACKWARD = 0, 1
 INPUT, CANDIDATE, OUTPUT = 0, 1, 2
 WARM_REPEATS = 4
-WARM_MATMULS = 4
+WARM_MATMULS = 3
 FLOPS = 2 * P * H * 3 * 2 * B
 
 BF16, F32, U16 = mybir.dt.bfloat16, mybir.dt.float32, mybir.dt.uint16

@@ -41,12 +41,24 @@ def tile_textbilstm_kernel(
         nc.sync.dma_start(offsets[:], offs)
         weights = {}
         biases = {}
-        for d, g in order:
-            w_dram, b_dram = in_dram[(d, g)]
+
+        def load_weights(d, g):
             weights[(d, g)] = held.tile([P, H], BF16, name=f"weight{d}{g}")
-            nc.sync.dma_start(weights[(d, g)][:], w_dram)
+            nc.sync.dma_start(weights[(d, g)][:], in_dram[(d, g)][0])
+
+        def load_bias(d, g):
             biases[(d, g)] = held.tile([P, BLOCKS], F32, name=f"bias{d}{g}")
-            nc.sync.dma_start(biases[(d, g)][:], b_dram.rearrange("(p k) o -> p (k o)", p=P))
+            nc.sync.dma_start(biases[(d, g)][:], in_dram[(d, g)][1].rearrange("(p k) o -> p (k o)", p=P))
+
+        first_three = order[:3]
+        load_weights(*first_three[0])
+        for d, g in first_three:
+            load_bias(d, g)
+        for d, g in first_three[1:]:
+            load_weights(d, g)
+        for d, g in order[3:]:
+            load_weights(d, g)
+            load_bias(d, g)
 
         zeros = held.tile([P, P], BF16, name="zeros")
         nc.vector.memset(zeros[:], 0.0)
@@ -69,12 +81,21 @@ def tile_textbilstm_kernel(
             (FORWARD, OUTPUT): shared[:, 1],
             (BACKWARD, OUTPUT): psum.tile([P, BLOCKS, B], F32, name="bank_o_bw"),
         }
-        for d, g in order:
+
+        def project(d, g, k):
+            looked_up = words[:].indirect(offsets[:, d * (B // 16) : (d + 1) * (B // 16)])
+            nc.tensor.matmul(
+                banks[(d, g)][:, k, :], weights[(d, g)][:, k::BLOCKS], looked_up, start=True, stop=True
+            )
+
+        for k in range(BLOCKS):
+            project(FORWARD, INPUT, k)
+        for k in range(BLOCKS):
+            project(FORWARD, CANDIDATE, k)
+            project(BACKWARD, INPUT, k)
+        for d, g in order[3:]:
             for k in range(BLOCKS):
-                looked_up = words[:].indirect(offsets[:, d * (B // 16) : (d + 1) * (B // 16)])
-                nc.tensor.matmul(
-                    banks[(d, g)][:, k, :], weights[(d, g)][:, k::BLOCKS], looked_up, start=True, stop=True
-                )
+                project(d, g, k)
 
         def squash(d, g):
             gate = {}

@@ -7,7 +7,7 @@ BLOCKS = H // P
 B = 128
 FORWARD, BACKWARD = 0, 1
 INPUT, CANDIDATE, OUTPUT = 0, 1, 2
-WARM_REPEATS = 4
+PIECES = 4
 WARM_MATMULS = 3
 FLOPS = 2 * P * H * 3 * 2 * B
 
@@ -56,44 +56,42 @@ def tile_textbilstm_kernel(
             load_bias(d, g)
         for d, g in first_three[1:]:
             load_weights(d, g)
-        for d, g in order[3:]:
+        for d, g in order[3:5]:
             load_weights(d, g)
+        for d, g in order[3:5]:
             load_bias(d, g)
+        load_weights(*order[5])
+        load_bias(*order[5])
+
+        banks = {}
+        for place, (d, g) in enumerate(order):
+            if place > 0 and order[place - 1][1] == CANDIDATE:
+                for k in range(BLOCKS):
+                    single = psum.tile([P, B], F32, name=f"bank{d}{g}{k}")
+                    banks[(d, g, k)] = single[:]
+            else:
+                whole = psum.tile([P, PIECES, B], F32, name=f"bank{d}{g}")
+                for k in range(BLOCKS):
+                    banks[(d, g, k)] = whole[:, k, :]
 
         zeros = held.tile([P, P], BF16, name="zeros")
         nc.vector.memset(zeros[:], 0.0)
-        warm = psum.tile([P, WARM_REPEATS, P], F32, name="warm")
         for step in range(WARM_MATMULS):
             nc.tensor.matmul(
-                warm[:], zeros[:], zeros[:].unsqueeze(1).to_broadcast([P, WARM_REPEATS, P]), start=True, stop=True
+                whole[:], zeros[:], zeros[:].unsqueeze(1).to_broadcast([P, PIECES, B]), start=True, stop=True
             )
 
         primer = held.tile([P, 1], F32, name="primer")
         nc.vector.memset(primer[:], 0.0)
         nc.scalar.activation(primer[:], primer[:], SIGMOID)
 
-        shared = psum.tile([P, 2, BLOCKS, B], F32, name="shared")
-        banks = {
-            (FORWARD, INPUT): psum.tile([P, BLOCKS, B], F32, name="bank_i_fw"),
-            (FORWARD, CANDIDATE): psum.tile([P, BLOCKS, B], F32, name="bank_c_fw"),
-            (BACKWARD, INPUT): psum.tile([P, BLOCKS, B], F32, name="bank_i_bw"),
-            (BACKWARD, CANDIDATE): shared[:, 0],
-            (FORWARD, OUTPUT): shared[:, 1],
-            (BACKWARD, OUTPUT): psum.tile([P, BLOCKS, B], F32, name="bank_o_bw"),
-        }
-
         def project(d, g, k):
             looked_up = words[:].indirect(offsets[:, d * (B // 16) : (d + 1) * (B // 16)])
             nc.tensor.matmul(
-                banks[(d, g)][:, k, :], weights[(d, g)][:, k::BLOCKS], looked_up, start=True, stop=True
+                banks[(d, g, k)], weights[(d, g)][:, k::BLOCKS], looked_up, start=True, stop=True
             )
 
-        for k in range(BLOCKS):
-            project(FORWARD, INPUT, k)
-        for k in range(BLOCKS):
-            project(FORWARD, CANDIDATE, k)
-            project(BACKWARD, INPUT, k)
-        for d, g in order[3:]:
+        for d, g in order:
             for k in range(BLOCKS):
                 project(d, g, k)
 
@@ -102,7 +100,7 @@ def tile_textbilstm_kernel(
             for k in range(BLOCKS):
                 gate[k] = held.tile([P, B], F32, name=f"gate{d}{g}{k}")
                 nc.scalar.activation(
-                    gate[k][:], banks[(d, g)][:, k, :], FUNCTION[g], bias=biases[(d, g)][:, k : k + 1]
+                    gate[k][:], banks[(d, g, k)], FUNCTION[g], bias=biases[(d, g)][:, k : k + 1]
                 )
             return gate
 

@@ -7,8 +7,9 @@ BLOCKS = H // P
 B = 128
 FORWARD, BACKWARD = 0, 1
 INPUT, CANDIDATE, OUTPUT = 0, 1, 2
-PIECES = 4
+WARM_REPEATS = 4
 WARM_MATMULS = 3
+PSUM_BANKS = 8
 FLOPS = 2 * P * H * 3 * 2 * B
 
 BF16, F32, U16 = mybir.dt.bfloat16, mybir.dt.float32, mybir.dt.uint16
@@ -33,7 +34,7 @@ def tile_textbilstm_kernel(
     )
     with (
         tc.tile_pool(name="held", bufs=1) as held,
-        tc.psum_pool(name="psum", bufs=1) as psum,
+        tc.psum_pool(name="psum", bufs=PSUM_BANKS) as psum,
     ):
         words = held.tile([P, V], BF16, name="words")
         nc.sync.dma_start(words[:], table)
@@ -63,46 +64,27 @@ def tile_textbilstm_kernel(
         load_weights(*order[5])
         load_bias(*order[5])
 
-        banks = {}
-        for place, (d, g) in enumerate(order):
-            if place > 0 and order[place - 1][1] == CANDIDATE:
-                for k in range(BLOCKS):
-                    single = psum.tile([P, B], F32, name=f"bank{d}{g}{k}")
-                    banks[(d, g, k)] = single[:]
-            else:
-                whole = psum.tile([P, PIECES, B], F32, name=f"bank{d}{g}")
-                for k in range(BLOCKS):
-                    banks[(d, g, k)] = whole[:, k, :]
-
         zeros = held.tile([P, P], BF16, name="zeros")
         nc.vector.memset(zeros[:], 0.0)
+        warm = psum.tile([P, WARM_REPEATS, P], F32, name="warm", tag="bank")
         for step in range(WARM_MATMULS):
             nc.tensor.matmul(
-                whole[:], zeros[:], zeros[:].unsqueeze(1).to_broadcast([P, PIECES, B]), start=True, stop=True
+                warm[:], zeros[:], zeros[:].unsqueeze(1).to_broadcast([P, WARM_REPEATS, P]), start=True, stop=True
             )
 
         primer = held.tile([P, 1], F32, name="primer")
         nc.vector.memset(primer[:], 0.0)
         nc.scalar.activation(primer[:], primer[:], SIGMOID)
 
-        def project(d, g, k):
-            looked_up = words[:].indirect(offsets[:, d * (B // 16) : (d + 1) * (B // 16)])
-            nc.tensor.matmul(
-                banks[(d, g, k)], weights[(d, g)][:, k::BLOCKS], looked_up, start=True, stop=True
-            )
-
-        for d, g in order:
+        def gate(d, g):
+            blocks = {}
             for k in range(BLOCKS):
-                project(d, g, k)
-
-        def squash(d, g):
-            gate = {}
-            for k in range(BLOCKS):
-                gate[k] = held.tile([P, B], F32, name=f"gate{d}{g}{k}")
-                nc.scalar.activation(
-                    gate[k][:], banks[(d, g, k)], FUNCTION[g], bias=biases[(d, g)][:, k : k + 1]
-                )
-            return gate
+                projection = psum.tile([P, B], F32, name=f"projection{d}{g}{k}", tag="bank")
+                looked_up = words[:].indirect(offsets[:, d * (B // 16) : (d + 1) * (B // 16)])
+                nc.tensor.matmul(projection[:], weights[(d, g)][:, k::BLOCKS], looked_up, start=True, stop=True)
+                blocks[k] = held.tile([P, B], F32, name=f"gate{d}{g}{k}")
+                nc.scalar.activation(blocks[k][:], projection[:], FUNCTION[g], bias=biases[(d, g)][:, k : k + 1])
+            return blocks
 
         def product(name, left, right):
             result = {}
@@ -118,21 +100,20 @@ def tile_textbilstm_kernel(
                 nc.scalar.activation(squashed[k][:], state[k][:], TANH)
             return squashed
 
-        gate_i_fw = squash(FORWARD, INPUT)
-        candidate_fw = squash(FORWARD, CANDIDATE)
+        gate_i_fw = gate(FORWARD, INPUT)
+        candidate_fw = gate(FORWARD, CANDIDATE)
         state_fw = product("state_fw", gate_i_fw, candidate_fw)
-        gate_i_bw = squash(BACKWARD, INPUT)
+        gate_i_bw = gate(BACKWARD, INPUT)
         squashed_fw = tanh_of("squashed_fw", state_fw)
-        candidate_bw = squash(BACKWARD, CANDIDATE)
+        candidate_bw = gate(BACKWARD, CANDIDATE)
         state_bw = product("state_bw", gate_i_bw, candidate_bw)
-        gate_o_fw = squash(FORWARD, OUTPUT)
+        gate_o_fw = gate(FORWARD, OUTPUT)
         hidden_fw = product("hidden_fw", gate_o_fw, squashed_fw)
         squashed_bw = tanh_of("squashed_bw", state_bw)
-        gate_o_bw = squash(BACKWARD, OUTPUT)
+        gate_o_bw = gate(BACKWARD, OUTPUT)
         hidden_bw = product("hidden_bw", gate_o_bw, squashed_bw)
-        hidden = {(FORWARD, 0): hidden_fw[0], (FORWARD, 1): hidden_fw[1], (BACKWARD, 0): hidden_bw[0], (BACKWARD, 1): hidden_bw[1]}
         out_by_block = out.rearrange("(p k) r -> p k r", p=P)
         for k in range(BLOCKS):
             both = held.tile([P, B], F32, name=f"both{k}")
-            nc.vector.tensor_add(both[:], hidden[(FORWARD, k)][:], hidden[(BACKWARD, k)][:])
+            nc.vector.tensor_add(both[:], hidden_fw[k][:], hidden_bw[k][:])
             nc.sync.dma_start(out_by_block[:, k, :], both[:])

@@ -7,8 +7,6 @@ BLOCKS = H // P
 B = 128
 FORWARD, BACKWARD = 0, 1
 INPUT, CANDIDATE, OUTPUT = 0, 1, 2
-WARM_REPEATS = 4
-WARM_MATMULS = 3
 PSUM_BANKS = 8
 FLOPS = 2 * P * H * 3 * 2 * B
 
@@ -63,14 +61,6 @@ def tile_textbilstm_kernel(
             load_bias(d, g)
         load_weights(*order[5])
         load_bias(*order[5])
-
-        zeros = held.tile([P, P], BF16, name="zeros")
-        nc.vector.memset(zeros[:], 0.0)
-        warm = psum.tile([P, WARM_REPEATS, P], F32, name="warm", tag="bank")
-        for step in range(WARM_MATMULS):
-            nc.tensor.matmul(
-                warm[:], zeros[:], zeros[:].unsqueeze(1).to_broadcast([P, WARM_REPEATS, P]), start=True, stop=True
-            )
 
         primer = held.tile([P, 1], F32, name="primer")
         nc.vector.memset(primer[:], 0.0)

import concourse.mybir as mybir

P = 128
V = 512
H = 256
BLOCKS = H // P
B = 128
FORWARD, BACKWARD = 0, 1
INPUT, CANDIDATE, OUTPUT = 0, 1, 2
PSUM_BANKS = 8
FLOPS = 2 * P * H * 3 * 2 * B

BF16, F32, U16 = mybir.dt.bfloat16, mybir.dt.float32, mybir.dt.uint16
SIGMOID = mybir.ActivationFunctionType.Sigmoid
TANH = mybir.ActivationFunctionType.Tanh
FUNCTION = {INPUT: SIGMOID, CANDIDATE: TANH, OUTPUT: SIGMOID}


def tile_textbilstm_kernel(
    tc,
    table, wi_fw, bi_fw, wc_fw, bc_fw, wo_fw, bo_fw, wi_bw, bi_bw, wc_bw, bc_bw, wo_bw, bo_bw, offs,
    out,
):
    nc = tc.nc
    in_dram = {
        (FORWARD, INPUT): (wi_fw, bi_fw), (FORWARD, CANDIDATE): (wc_fw, bc_fw), (FORWARD, OUTPUT): (wo_fw, bo_fw),
        (BACKWARD, INPUT): (wi_bw, bi_bw), (BACKWARD, CANDIDATE): (wc_bw, bc_bw), (BACKWARD, OUTPUT): (wo_bw, bo_bw),
    }
    order = (
        (FORWARD, INPUT), (FORWARD, CANDIDATE), (BACKWARD, INPUT), (BACKWARD, CANDIDATE),
        (FORWARD, OUTPUT), (BACKWARD, OUTPUT),
    )
    with (
        tc.tile_pool(name="held", bufs=1) as held,
        tc.psum_pool(name="psum", bufs=PSUM_BANKS) as psum,
    ):
        words = held.tile([P, V], BF16, name="words")
        nc.sync.dma_start(words[:], table)
        offsets = held.tile([P, 2 * B // 16], U16, name="offsets")
        nc.sync.dma_start(offsets[:], offs)
        weights = {}
        biases = {}

        def load_weights(d, g):
            weights[(d, g)] = held.tile([P, H], BF16, name=f"weight{d}{g}")
            nc.sync.dma_start(weights[(d, g)][:], in_dram[(d, g)][0])

        def load_bias(d, g):
            biases[(d, g)] = held.tile([P, BLOCKS], F32, name=f"bias{d}{g}")
            nc.sync.dma_start(biases[(d, g)][:], in_dram[(d, g)][1].rearrange("(p k) o -> p (k o)", p=P))

        first_three = order[:3]
        load_weights(*first_three[0])
        for d, g in first_three:
            load_bias(d, g)
        for d, g in first_three[1:]:
            load_weights(d, g)
        for d, g in order[3:5]:
            load_weights(d, g)
        for d, g in order[3:5]:
            load_bias(d, g)
        load_weights(*order[5])
        load_bias(*order[5])

        primer = held.tile([P, 1], F32, name="primer")
        nc.vector.memset(primer[:], 0.0)
        nc.scalar.activation(primer[:], primer[:], SIGMOID)

        def gate(d, g):
            blocks = {}
            for k in range(BLOCKS):
                projection = psum.tile([P, B], F32, name=f"projection{d}{g}{k}", tag="bank")
                looked_up = words[:].indirect(offsets[:, d * (B // 16) : (d + 1) * (B // 16)])
                nc.tensor.matmul(projection[:], weights[(d, g)][:, k::BLOCKS], looked_up, start=True, stop=True)
                blocks[k] = held.tile([P, B], F32, name=f"gate{d}{g}{k}")
                nc.scalar.activation(blocks[k][:], projection[:], FUNCTION[g], bias=biases[(d, g)][:, k : k + 1])
            return blocks

        def product(name, left, right):
            result = {}
            for k in range(BLOCKS):
                result[k] = held.tile([P, B], F32, name=f"{name}{k}")
                nc.vector.tensor_mul(result[k][:], left[k][:], right[k][:])
            return result

        def tanh_of(name, state):
            squashed = {}
            for k in range(BLOCKS):
                squashed[k] = held.tile([P, B], F32, name=f"{name}{k}")
                nc.scalar.activation(squashed[k][:], state[k][:], TANH)
            return squashed

        gate_i_fw = gate(FORWARD, INPUT)
        candidate_fw = gate(FORWARD, CANDIDATE)
        state_fw = product("state_fw", gate_i_fw, candidate_fw)
        gate_i_bw = gate(BACKWARD, INPUT)
        squashed_fw = tanh_of("squashed_fw", state_fw)
        candidate_bw = gate(BACKWARD, CANDIDATE)
        state_bw = product("state_bw", gate_i_bw, candidate_bw)
        gate_o_fw = gate(FORWARD, OUTPUT)
        hidden_fw = product("hidden_fw", gate_o_fw, squashed_fw)
        squashed_bw = tanh_of("squashed_bw", state_bw)
        gate_o_bw = gate(BACKWARD, OUTPUT)
        hidden_bw = product("hidden_bw", gate_o_bw, squashed_bw)
        out_by_block = out.rearrange("(p k) r -> p k r", p=P)
        for k in range(BLOCKS):
            both = held.tile([P, B], F32, name=f"both{k}")
            nc.vector.tensor_add(both[:], hidden_fw[k][:], hidden_bw[k][:])
            nc.sync.dma_start(out_by_block[:, k, :], both[:])
